import numpy as np
import ml_dtypes


def mxq(x, axis, fmt="e4m3"):
    dtype, down = {"e4m3": (ml_dtypes.float8_e4m3fn, 7), "e5m2": (ml_dtypes.float8_e5m2, 14)}[fmt]
    v = np.moveaxis(np.asarray(x, np.float32).astype(ml_dtypes.bfloat16).astype(np.float64), axis, -1)
    blocks = v.reshape(v.shape[:-1] + (-1, 32))
    amax = np.abs(blocks).max(-1, keepdims=True)
    byte = np.maximum(np.where(amax > 0, np.frexp(amax)[1] - 1 + 127, 0) - down, 1)
    scale = np.exp2(byte - 127.0)
    codes = (blocks / scale).astype(np.float32).astype(dtype).astype(np.float64)
    return np.moveaxis((codes * scale).reshape(v.shape), -1, axis)


WIDE = False


def mx_kscale(k):
    if not WIDE:
        return np.ones(k)
    levels = np.array([10, -10, 5, -5, 0])
    if k % 512:
        return np.exp2(np.random.permutation(np.resize(levels, k // 32))).repeat(32)
    a = np.empty((k // 512, 16))
    for p in range(k // 512):
        a[p, :8] = np.random.permutation(np.resize(levels, 8))
        for g in range(8):
            far = levels[np.abs(levels - a[p, g]) >= 10]
            a[p, g + 8] = far[np.random.randint(len(far))]
    return np.exp2(a.ravel()).repeat(32)


BF16 = ml_dtypes.bfloat16


def bf(x):
    return np.asarray(x, np.float32).astype(BF16)


def f64(x):
    return np.asarray(x).astype(np.float64)


B, P0, P1, P2, K0, K1, K2 = 128, 4096, 9216, 7168, 512, 512, 512
PT = P0 + P1 + P2
KT = K0 + K1 + K2
CLIP0 = 1.0


def clip_rows(mat, clip):
    norms = np.sqrt(np.sum(mat * mat, axis=1, keepdims=True))
    scale = np.minimum(clip / norms, 1.0)
    return mat * scale


def draw0():
    s0, s1, s2 = mx_kscale(P0), mx_kscale(P1), mx_kscale(P2)
    r = np.exp2(np.random.uniform(-2.0, 2.0, (B, 1))) / (KT * PT) ** 0.25
    return {"target_grad": bf(np.random.standard_normal((B, PT)) * r * np.concatenate([s0, s1, s2])),
            "bases0": bf(np.random.standard_normal((P0, K0)) / np.sqrt(P0) / s0[:, None]),
            "bases1": bf(np.random.standard_normal((P1, K1)) / np.sqrt(P1) / s1[:, None]),
            "bases2": bf(np.random.standard_normal((P2, K2)) / np.sqrt(P2) / s2[:, None])}


def core(target_grad, bases0, bases1, bases2):
    g = f64(target_grad)
    embeddings = []
    offset = 0
    for b in (f64(bases0), f64(bases1), f64(bases2)):
        num_p = b.shape[0]
        embeddings.append(mxq(g[:, offset:offset + num_p], 1, "e4m3") @ mxq(b, 0, "e4m3"))
        offset += num_p
    embedding = np.concatenate(embeddings, axis=1)
    avg_clipped_embedding = np.sum(clip_rows(embedding, CLIP0), axis=0) / B
    return embedding, avg_clipped_embedding


def e4m3fn_bytes(y):
    return np.clip(np.asarray(y, np.float64), -448.0, 448.0).astype(np.float32).astype(ml_dtypes.float8_e4m3fn).view(np.uint8)


def e4m3fn_values(b):
    return np.asarray(b, np.uint8).view(ml_dtypes.float8_e4m3fn).astype(np.float64)


def setup_inputs():
    d = draw0()
    x0 = np.asarray(d['bases1']).astype(np.float64)
    s = (np.max(np.abs(x0), axis=(1,), keepdims=True) / 448.0).astype(np.float32)
    out = {}
    for k, v in d.items():
        if k == 'bases1':
            out['bases1_bytes'] = e4m3fn_bytes(x0 / s.astype(np.float64))
            out['bases1_scale'] = s
        else:
            out[k] = v
    return out


def reference(target_grad, bases0, bases1_bytes, bases1_scale, bases2):
    return core(target_grad, bases0, e4m3fn_values(bases1_bytes) * bases1_scale.astype(np.float64), bases2)

@@ -1,0 +1,255 @@
+from contextlib import ExitStack
+
+import concourse.mybir as mybir
+from concourse.masks import make_identity
+
+F32 = mybir.dt.float32
+BF16 = mybir.dt.bfloat16
+U32 = mybir.dt.uint32
+U8 = mybir.dt.uint8
+FP8 = mybir.dt.float8_e4m3fn
+FP8X4 = mybir.dt.float8_e4m3fn_x4
+ACT = mybir.ActivationFunctionType
+ALU = mybir.AluOpType
+
+P = 128
+PACK = 4
+K_PASS = P * PACK
+N = 512
+W = PACK * N
+GROUP_FIRST = (0, 8, 26)
+GROUP_PASSES = (8, 18, 14)
+N_PASS = 40
+BLK = 4
+FLOPS = 2 * 128 * 20480 * 512
+
+SCALAR_INTERLEAVES = (6, 14, 22, 30, 36, 38)
+LOOKAHEAD = 6
+
+
+def pass_order():
+    plain = list(range(0, 8)) + list(range(26, 40))
+    coded = list(range(8, 26))
+    order = []
+    for i in range(len(coded)):
+        order.append(plain[i])
+        order.append(coded[i])
+    order.extend(plain[len(coded):])
+    return order
+
+
+def group_of(gp):
+    x = 0
+    for g in range(3):
+        if gp >= GROUP_FIRST[g]:
+            x = g
+    return x, gp - GROUP_FIRST[x]
+
+
+def tile_gep_pa_kernel(tc, target_grad, bases0, bases1_bytes, bases1_scale, bases2, out_0, out_1):
+    nc = tc.nc
+    order = pass_order()
+    first_need = {}
+    for s, gp in enumerate(order):
+        first_need.setdefault(gp // BLK, s)
+
+    events = []
+    for s, gp in enumerate(order):
+        events.append((float(s), 0, gp))
+    for blk, s in first_need.items():
+        events.append((s + 2.5, 1, blk))
+    events = sorted(events)
+
+    with ExitStack() as ctx:
+        const = ctx.enter_context(tc.tile_pool(name="const", bufs=1))
+        braw_pool = ctx.enter_context(tc.tile_pool(name="braw", bufs=6))
+        byte_pool = ctx.enter_context(tc.tile_pool(name="bytes", bufs=6))
+        graw_pool = ctx.enter_context(tc.tile_pool(name="graw", bufs=3))
+        wid_pool = ctx.enter_context(tc.tile_pool(name="wid", bufs=3))
+        grp_pool = ctx.enter_context(tc.tile_pool(name="grp", bufs=4))
+        cq_pool = ctx.enter_context(tc.tile_pool(name="cq", bufs=6))
+        ggrp_pool = ctx.enter_context(tc.tile_pool(name="ggrp", bufs=2))
+        gq_pool = ctx.enter_context(tc.tile_pool(name="gq", bufs=1))
+        psum_acc = ctx.enter_context(tc.psum_pool(name="psacc", bufs=1))
+        psum_t = ctx.enter_context(tc.psum_pool(name="pst", bufs=4))
+
+        sc = const.tile([P, 72], F32, name="sc")
+        with nc.allow_non_contiguous_dma(reason="16-byte runs of scales"):
+            nc.scalar.dma_start(
+                out=sc[:].rearrange("p (g t) -> p g t", t=PACK),
+                in_=bases1_scale.rearrange("(g p t) o -> p g (t o)", p=P, t=PACK),
+            )
+        one = const.tile([P, 1], F32, name="one")
+        nc.vector.memset(one[:], 1.0)
+        warm = const.tile([P, 1], F32, name="warm")
+        nc.scalar.activation(out=warm[:], in_=one[:], func=ACT.Sqrt)
+        ident = const.tile([P, P], F32, name="ident")
+        make_identity(nc, ident[:])
+
+        e_sb = const.tile([P, 3 * N], F32, name="e_sb")
+        avg_sb = const.tile([P, 3 * N], F32, name="avg_sb")
+        junk = const.tile([P, N], F32, name="junk")
+        ss = const.tile([P, 4], F32, name="ss")
+        acc = []
+        for x in range(3):
+            acc_x = psum_acc.tile([P, N], F32, name="acc%d" % x)
+            acc.append(acc_x)
+
+        raw = {}
+        graw = {}
+        xts = {}
+        ggrps = {}
+        gcodes = {}
+        wids = {}
+        grps = {}
+        codes = {}
+
+        def load(kind, idx):
+            if kind == 1:
+                t = graw_pool.tile([P, BLK * K_PASS], BF16, name="graw")
+                nc.sync.dma_start(out=t[:], in_=target_grad[:, idx * BLK * K_PASS:(idx + 1) * BLK * K_PASS])
+                graw[idx] = t
+                return
+            x, l = group_of(idx)
+            rows = slice(l * K_PASS, (l + 1) * K_PASS)
+            if x == 1:
+                t = byte_pool.tile([P, W], U8, name="b1bytes")
+                nc.sync.dma_start(out=t[:], in_=bases1_bytes[rows, :].rearrange("(p j) n -> p (j n)", j=PACK))
+            else:
+                src = bases0 if x == 0 else bases2
+                t = braw_pool.tile([P, W], BF16, name="braw")
+                nc.sync.dma_start(out=t[:], in_=src[rows, :].rearrange("(p j) n -> p (j n)", j=PACK))
+            raw[idx] = t
+
+        def transposes(blk):
+            words = graw[blk][:].bitcast(F32)
+            banks = []
+            for h in range(2):
+                xt = psum_t.tile([P, N], F32, name="xt")
+                for a in range(2):
+                    for u in range(2):
+                        base = 256 * (2 * h + a)
+                        nc.tensor.transpose(
+                            out=xt[:, (2 * a + u) * P:(2 * a + u + 1) * P],
+                            in_=words[:, base + u:base + 256:2],
+                            identity=ident[:],
+                        )
+                banks.append(xt)
+            xts[blk] = banks
+
+        def evacuate(blk):
+            ggrp = ggrp_pool.tile([P, BLK * K_PASS], BF16, name="ggrp", align_bytes=64)
+            for h in range(2):
+                nc.scalar.copy(
+                    out=ggrp[:, h * 1024:(h + 1) * 1024].bitcast(F32).rearrange("p (a r u) -> p a r u", a=2, u=2),
+                    in_=xts[blk][h][:].rearrange("p (a u r) -> p a r u", a=2, u=2),
+                )
+            ggrps[blk] = ggrp
+
+        def quantize_g(blk):
+            gc = gq_pool.tile([P, BLK * P], U32, name="gc%d" % blk, align_bytes=64)
+            gs = gq_pool.tile([P, BLK * P], U8, name="gs%d" % blk, align_bytes=64)
+            nc.vector.quantize_mx(out=gc[:].bitcast(FP8X4), scales=gs[:], in_=ggrps[blk][:])
+            gcodes[blk] = (gc, gs)
+
+        def widen(s):
+            gp = order[s]
+            x, l = group_of(gp)
+            if x != 1:
+                return
+            wid = wid_pool.tile([P, W], BF16, name="wid")
+            for j in range(PACK):
+                nc.scalar.activation(
+                    out=wid[:, j * N:(j + 1) * N],
+                    in_=raw[gp][:, j * N:(j + 1) * N].bitcast(FP8),
+                    func=ACT.Copy,
+                    scale=sc[:, l * PACK + j:l * PACK + j + 1],
+                )
+            wids[s] = wid
+
+        def interleave(s):
+            gp = order[s]
+            src = wids[s] if s in wids else raw[gp]
+            grp = grp_pool.tile([P, W], BF16, name="grp", align_bytes=64)
+            dst_v = grp[:].rearrange("p (c i t) -> p c t i", i=4, t=PACK)
+            src_v = src[:].rearrange("p (t c i) -> p c t i", t=PACK, i=4)
+            if s in SCALAR_INTERLEAVES:
+                nc.scalar.copy(out=dst_v, in_=src_v)
+            else:
+                nc.vector.tensor_copy(out=dst_v, in_=src_v)
+            grps[s] = grp
+
+        def quantize(s):
+            cd = cq_pool.tile([P, N], U32, name="codes", align_bytes=64)
+            sl = cq_pool.tile([P, N], U8, name="scales", align_bytes=64)
+            nc.vector.quantize_mx(out=cd[:].bitcast(FP8X4), scales=sl[:], in_=grps[s][:])
+            codes[s] = (cd, sl)
+
+        def finish_group(x):
+            cols = slice(x * N, (x + 1) * N)
+            nc.scalar.activation(out=junk[:], in_=acc[x][:], func=ACT.Square, accum_out=ss[:, x:x + 1])
+            if x == 2:
+                nc.scalar.copy(out=e_sb[:, cols], in_=acc[x][:])
+                nc.sync.dma_start(out=out_0[:, cols], in_=e_sb[:, cols])
+            else:
+                nc.vector.tensor_copy(out=e_sb[:, cols], in_=acc[x][:])
+                nc.gpsimd.dma_start(out=out_0[:, cols], in_=e_sb[:, cols])
+
+        def multiply(s):
+            gp = order[s]
+            x, l = group_of(gp)
+            gc, gs = gcodes[gp // BLK]
+            a = gp % BLK
+            cd, sl = codes[s]
+            nc.tensor.matmul_mx(
+                out=acc[x][:],
+                lhsT=gc[:, a * P:(a + 1) * P].bitcast(FP8X4),
+                lhsT_scale=gs[:, a * P:(a + 1) * P],
+                rhs=cd[:].bitcast(FP8X4),
+                rhs_scale=sl[:],
+                start=(l == 0),
+                stop=(l == GROUP_PASSES[x] - 1),
+            )
+            if l == GROUP_PASSES[x] - 1:
+                finish_group(x)
+
+        for it in range(-LOOKAHEAD, N_PASS + 2):
+            for when, kind, idx in events:
+                if int(when) - LOOKAHEAD == it:
+                    load(kind, idx)
+            for blk, s in first_need.items():
+                if s == it + 4:
+                    transposes(blk)
+            for blk, s in first_need.items():
+                if s == it + 3:
+                    evacuate(blk)
+            if 0 <= it + 2 < N_PASS:
+                widen(it + 2)
+            if 0 <= it + 1 < N_PASS:
+                interleave(it + 1)
+            if 0 <= it < N_PASS:
+                quantize(it)
+            for blk, s in first_need.items():
+                if s == it + 2:
+                    quantize_g(blk)
+            if 0 <= it - 1 < N_PASS:
+                multiply(it - 1)
+
+        ss01 = const.tile([P, 1], F32, name="ss01")
+        nc.vector.tensor_tensor(out=ss01[:], in0=ss[:, 0:1], in1=ss[:, 1:2], op=ALU.add)
+        m = const.tile([P, 1], F32, name="m")
+        nc.vector.tensor_scalar(out=m[:], in0=ss[:, 2:3], scalar1=ss01[:, 0:1], scalar2=1.0, op0=ALU.add, op1=ALU.max)
+        n128 = const.tile([P, 1], F32, name="n128")
+        nc.scalar.activation(out=n128[:], in_=m[:], func=ACT.Sqrt, scale=16384.0)
+        cw = const.tile([P, 1], F32, name="cw")
+        nc.vector.reciprocal(out=cw[:], in_=n128[:])
+        out_1_row = out_1.rearrange("(o n) -> o n", o=1)
+        for x in range(3):
+            cols = slice(x * N, (x + 1) * N)
+            ps = psum_t.tile([P, N], F32, name="xt")
+            nc.tensor.matmul(out=ps[:], lhsT=cw[:, 0:1].to_broadcast([P, P]), rhs=e_sb[:, cols], start=True, stop=True)
+            if x == 1:
+                nc.scalar.copy(out=avg_sb[0:1, cols], in_=ps[0:1, :])
+            else:
+                nc.vector.tensor_copy(out=avg_sb[0:1, cols], in_=ps[0:1, :])
+            nc.sync.dma_start(out=out_1_row[:, cols], in_=avg_sb[0:1, cols])

@@ -23,18 +23,21 @@ N_PASS = 40
 BLK = 4
 FLOPS = 2 * 128 * 20480 * 512
 
-SCALAR_INTERLEAVES = (6, 14, 22, 30, 36, 38)
-LOOKAHEAD = 6
+SCALAR_INTERLEAVES = (12, 20, 28, 34, 38, 39)
+LOOKAHEAD = 8
+LEAD = 3
+WARMERS = {33: 2, 34: 2, 35: 2, 39: 4}
 
 
 def pass_order():
     plain = list(range(0, 8)) + list(range(26, 40))
     coded = list(range(8, 26))
-    order = []
+    order = plain[:LEAD]
+    rest = plain[LEAD:]
     for i in range(len(coded)):
-        order.append(plain[i])
         order.append(coded[i])
-    order.extend(plain[len(coded):])
+        order.append(rest[i])
+    order.extend(rest[len(coded):])
     return order
 
 
@@ -57,7 +60,7 @@ def tile_gep_pa_kernel(tc, target_grad, bases0, bases1_bytes, bases1_scale, base
     for s, gp in enumerate(order):
         events.append((float(s), 0, gp))
     for blk, s in first_need.items():
-        events.append((s + 2.5, 1, blk))
+        events.append((s + 0.5, 1, blk))
     events = sorted(events)
 
     with ExitStack() as ctx:
@@ -66,12 +69,13 @@ def tile_gep_pa_kernel(tc, target_grad, bases0, bases1_bytes, bases1_scale, base
         byte_pool = ctx.enter_context(tc.tile_pool(name="bytes", bufs=6))
         graw_pool = ctx.enter_context(tc.tile_pool(name="graw", bufs=3))
         wid_pool = ctx.enter_context(tc.tile_pool(name="wid", bufs=3))
-        grp_pool = ctx.enter_context(tc.tile_pool(name="grp", bufs=4))
-        cq_pool = ctx.enter_context(tc.tile_pool(name="cq", bufs=6))
+        grp_pool = ctx.enter_context(tc.tile_pool(name="grp", bufs=5))
+        cq_pool = ctx.enter_context(tc.tile_pool(name="cq", bufs=8))
         ggrp_pool = ctx.enter_context(tc.tile_pool(name="ggrp", bufs=2))
         gq_pool = ctx.enter_context(tc.tile_pool(name="gq", bufs=1))
         psum_acc = ctx.enter_context(tc.psum_pool(name="psacc", bufs=1))
         psum_t = ctx.enter_context(tc.psum_pool(name="pst", bufs=4))
+        psum_w = ctx.enter_context(tc.psum_pool(name="psw", bufs=1))
 
         sc = const.tile([P, 72], F32, name="sc")
         with nc.allow_non_contiguous_dma(reason="16-byte runs of scales"):
@@ -82,7 +86,10 @@ def tile_gep_pa_kernel(tc, target_grad, bases0, bases1_bytes, bases1_scale, base
         one = const.tile([P, 1], F32, name="one")
         nc.vector.memset(one[:], 1.0)
         warm = const.tile([P, 1], F32, name="warm")
-        nc.scalar.activation(out=warm[:], in_=one[:], func=ACT.Sqrt)
+        nc.scalar.activation(out=warm[:], in_=one[:], func=ACT.Abs_reciprocal_sqrt)
+        zeros = const.tile([P, N], BF16, name="zeros")
+        nc.vector.memset(zeros[:], 0.0)
+        idle_ps = psum_w.tile([P, N], F32, name="idle_ps")
         ident = const.tile([P, P], F32, name="ident")
         make_identity(nc, ident[:])
 
@@ -188,10 +195,7 @@ def tile_gep_pa_kernel(tc, target_grad, bases0, bases1_bytes, bases1_scale, base
         def finish_group(x):
             cols = slice(x * N, (x + 1) * N)
             nc.scalar.activation(out=junk[:], in_=acc[x][:], func=ACT.Square, accum_out=ss[:, x:x + 1])
-            if x == 2:
-                nc.scalar.copy(out=e_sb[:, cols], in_=acc[x][:])
-                nc.sync.dma_start(out=out_0[:, cols], in_=e_sb[:, cols])
-            else:
+            if x != 2:
                 nc.vector.tensor_copy(out=e_sb[:, cols], in_=acc[x][:])
                 nc.gpsimd.dma_start(out=out_0[:, cols], in_=e_sb[:, cols])
 
@@ -212,37 +216,42 @@ def tile_gep_pa_kernel(tc, target_grad, bases0, bases1_bytes, bases1_scale, base
             )
             if l == GROUP_PASSES[x] - 1:
                 finish_group(x)
+            for w in range(WARMERS.get(s, 0)):
+                nc.tensor.matmul(out=idle_ps[:], lhsT=zeros[:, 0:P], rhs=zeros[:], start=True, stop=True)
 
-        for it in range(-LOOKAHEAD, N_PASS + 2):
+        ctx.enter_context(tc.manual_schedule())
+        for it in range(-LOOKAHEAD, N_PASS + 4):
             for when, kind, idx in events:
                 if int(when) - LOOKAHEAD == it:
                     load(kind, idx)
             for blk, s in first_need.items():
-                if s == it + 4:
+                if s == it + 2:
                     transposes(blk)
-            for blk, s in first_need.items():
-                if s == it + 3:
-                    evacuate(blk)
             if 0 <= it + 2 < N_PASS:
                 widen(it + 2)
-            if 0 <= it + 1 < N_PASS:
+            for blk, s in first_need.items():
+                if s == it:
+                    evacuate(blk)
+            if 0 <= it + 2 < N_PASS and it + 2 in SCALAR_INTERLEAVES:
+                interleave(it + 2)
+            if 0 <= it + 1 < N_PASS and it + 1 not in SCALAR_INTERLEAVES:
                 interleave(it + 1)
             if 0 <= it < N_PASS:
                 quantize(it)
             for blk, s in first_need.items():
-                if s == it + 2:
+                if s == it - 1:
                     quantize_g(blk)
-            if 0 <= it - 1 < N_PASS:
-                multiply(it - 1)
+            if 0 <= it - 4 < N_PASS:
+                multiply(it - 4)
 
         ss01 = const.tile([P, 1], F32, name="ss01")
         nc.vector.tensor_tensor(out=ss01[:], in0=ss[:, 0:1], in1=ss[:, 1:2], op=ALU.add)
         m = const.tile([P, 1], F32, name="m")
         nc.vector.tensor_scalar(out=m[:], in0=ss[:, 2:3], scalar1=ss01[:, 0:1], scalar2=1.0, op0=ALU.add, op1=ALU.max)
-        n128 = const.tile([P, 1], F32, name="n128")
-        nc.scalar.activation(out=n128[:], in_=m[:], func=ACT.Sqrt, scale=16384.0)
         cw = const.tile([P, 1], F32, name="cw")
-        nc.vector.reciprocal(out=cw[:], in_=n128[:])
+        nc.scalar.activation(out=cw[:], in_=m[:], func=ACT.Abs_reciprocal_sqrt, scale=16384.0)
+        nc.scalar.copy(out=e_sb[:, 2 * N:3 * N], in_=acc[2][:])
+        nc.sync.dma_start(out=out_0[:, 2 * N:3 * N], in_=e_sb[:, 2 * N:3 * N])
         out_1_row = out_1.rearrange("(o n) -> o n", o=1)
         for x in range(3):
             cols = slice(x * N, (x + 1) * N)

@@ -23,10 +23,12 @@ N_PASS = 40
 BLK = 4
 FLOPS = 2 * 128 * 20480 * 512
 
-SCALAR_INTERLEAVES = (12, 20, 28, 34, 38, 39)
+SCALAR_INTERLEAVES = (9, 17, 25, 31, 35, 37, 38)
 LOOKAHEAD = 8
-LEAD = 3
-WARMERS = {33: 2, 34: 2, 35: 2, 39: 4}
+LEAD = 2
+SC_FIRST = 4
+SC_REST_AFTER = 6
+WARMERS = {33: 2, 34: 2, 35: 2, 39: 3}
 
 
 def pass_order():
@@ -58,9 +60,9 @@ def tile_gep_pa_kernel(tc, target_grad, bases0, bases1_bytes, bases1_scale, base
 
     events = []
     for s, gp in enumerate(order):
-        events.append((float(s), 0, gp))
+        events.append((s - (1.2 if group_of(gp)[0] == 1 else 0.0), 0, gp))
     for blk, s in first_need.items():
-        events.append((s + 0.5, 1, blk))
+        events.append((s + 1.5, 1, blk))
     events = sorted(events)
 
     with ExitStack() as ctx:
@@ -68,21 +70,18 @@ def tile_gep_pa_kernel(tc, target_grad, bases0, bases1_bytes, bases1_scale, base
         braw_pool = ctx.enter_context(tc.tile_pool(name="braw", bufs=6))
         byte_pool = ctx.enter_context(tc.tile_pool(name="bytes", bufs=6))
         graw_pool = ctx.enter_context(tc.tile_pool(name="graw", bufs=3))
-        wid_pool = ctx.enter_context(tc.tile_pool(name="wid", bufs=3))
+        wid_pool = ctx.enter_context(tc.tile_pool(name="wid", bufs=4))
         grp_pool = ctx.enter_context(tc.tile_pool(name="grp", bufs=5))
-        cq_pool = ctx.enter_context(tc.tile_pool(name="cq", bufs=8))
+        cq_pool = ctx.enter_context(tc.tile_pool(name="cq", bufs=10))
         ggrp_pool = ctx.enter_context(tc.tile_pool(name="ggrp", bufs=2))
         gq_pool = ctx.enter_context(tc.tile_pool(name="gq", bufs=1))
         psum_acc = ctx.enter_context(tc.psum_pool(name="psacc", bufs=1))
         psum_t = ctx.enter_context(tc.psum_pool(name="pst", bufs=4))
         psum_w = ctx.enter_context(tc.psum_pool(name="psw", bufs=1))
 
-        sc = const.tile([P, 72], F32, name="sc")
-        with nc.allow_non_contiguous_dma(reason="16-byte runs of scales"):
-            nc.scalar.dma_start(
-                out=sc[:].rearrange("p (g t) -> p g t", t=PACK),
-                in_=bases1_scale.rearrange("(g p t) o -> p g (t o)", p=P, t=PACK),
-            )
+        scale_view = bases1_scale.rearrange("(g p t) o -> p g (t o)", p=P, t=PACK)
+        sc_a = const.tile([P, SC_FIRST * PACK], F32, name="sc_a")
+        sc_b = const.tile([P, (GROUP_PASSES[1] - SC_FIRST) * PACK], F32, name="sc_b")
         one = const.tile([P, 1], F32, name="one")
         nc.vector.memset(one[:], 1.0)
         warm = const.tile([P, 1], F32, name="warm")
@@ -170,7 +169,8 @@ def tile_gep_pa_kernel(tc, target_grad, bases0, bases1_bytes, bases1_scale, base
                     out=wid[:, j * N:(j + 1) * N],
                     in_=raw[gp][:, j * N:(j + 1) * N].bitcast(FP8),
                     func=ACT.Copy,
-                    scale=sc[:, l * PACK + j:l * PACK + j + 1],
+                    scale=(sc_a[:, l * PACK + j:l * PACK + j + 1] if l < SC_FIRST
+                           else sc_b[:, (l - SC_FIRST) * PACK + j:(l - SC_FIRST) * PACK + j + 1]),
                 )
             wids[s] = wid
 
@@ -197,7 +197,8 @@ def tile_gep_pa_kernel(tc, target_grad, bases0, bases1_bytes, bases1_scale, base
             nc.scalar.activation(out=junk[:], in_=acc[x][:], func=ACT.Square, accum_out=ss[:, x:x + 1])
             if x != 2:
                 nc.vector.tensor_copy(out=e_sb[:, cols], in_=acc[x][:])
-                nc.gpsimd.dma_start(out=out_0[:, cols], in_=e_sb[:, cols])
+            if x == 1:
+                nc.sync.dma_start(out=out_0[:, 0:2 * N], in_=e_sb[:, 0:2 * N])
 
         def multiply(s):
             gp = order[s]
@@ -220,17 +221,25 @@ def tile_gep_pa_kernel(tc, target_grad, bases0, bases1_bytes, bases1_scale, base
                 nc.tensor.matmul(out=idle_ps[:], lhsT=zeros[:, 0:P], rhs=zeros[:], start=True, stop=True)
 
         ctx.enter_context(tc.manual_schedule())
-        for it in range(-LOOKAHEAD, N_PASS + 4):
-            for when, kind, idx in events:
-                if int(when) - LOOKAHEAD == it:
+        for it in range(-LOOKAHEAD - 2, N_PASS + 4):
+            for e_i, (when, kind, idx) in enumerate(events):
+                if int(when + 100) - 100 - LOOKAHEAD == it:
                     load(kind, idx)
+                    if e_i == 0:
+                        with nc.allow_non_contiguous_dma(reason="16-byte runs of scales"):
+                            nc.sync.dma_start(out=sc_a[:].rearrange("p (g t) -> p g t", t=PACK),
+                                              in_=scale_view[:, 0:SC_FIRST, :])
+                    if e_i == SC_REST_AFTER:
+                        with nc.allow_non_contiguous_dma(reason="16-byte runs of scales"):
+                            nc.sync.dma_start(out=sc_b[:].rearrange("p (g t) -> p g t", t=PACK),
+                                              in_=scale_view[:, SC_FIRST:GROUP_PASSES[1], :])
             for blk, s in first_need.items():
                 if s == it + 2:
                     transposes(blk)
-            if 0 <= it + 2 < N_PASS:
-                widen(it + 2)
+            if 0 <= it + 3 < N_PASS:
+                widen(it + 3)
             for blk, s in first_need.items():
-                if s == it:
+                if s == it - 1:
                     evacuate(blk)
             if 0 <= it + 2 < N_PASS and it + 2 in SCALAR_INTERLEAVES:
                 interleave(it + 2)
@@ -239,7 +248,7 @@ def tile_gep_pa_kernel(tc, target_grad, bases0, bases1_bytes, bases1_scale, base
             if 0 <= it < N_PASS:
                 quantize(it)
             for blk, s in first_need.items():
-                if s == it - 1:
+                if s == it - 2:
                     quantize_g(blk)
             if 0 <= it - 4 < N_PASS:
                 multiply(it - 4)
@@ -253,12 +262,13 @@ def tile_gep_pa_kernel(tc, target_grad, bases0, bases1_bytes, bases1_scale, base
         nc.scalar.copy(out=e_sb[:, 2 * N:3 * N], in_=acc[2][:])
         nc.sync.dma_start(out=out_0[:, 2 * N:3 * N], in_=e_sb[:, 2 * N:3 * N])
         out_1_row = out_1.rearrange("(o n) -> o n", o=1)
-        for x in range(3):
-            cols = slice(x * N, (x + 1) * N)
+        pieces = ((0, N), (N, N), (2 * N, N // 2), (2 * N + N // 2, N // 2))
+        for i, (c0, width) in enumerate(pieces):
+            cols = slice(c0, c0 + width)
             ps = psum_t.tile([P, N], F32, name="xt")
-            nc.tensor.matmul(out=ps[:], lhsT=cw[:, 0:1].to_broadcast([P, P]), rhs=e_sb[:, cols], start=True, stop=True)
-            if x == 1:
-                nc.scalar.copy(out=avg_sb[0:1, cols], in_=ps[0:1, :])
+            nc.tensor.matmul(out=ps[:, 0:width], lhsT=cw[:, 0:1].to_broadcast([P, P]), rhs=e_sb[:, cols], start=True, stop=True)
+            if i % 2 == 1:
+                nc.scalar.copy(out=avg_sb[0:1, cols], in_=ps[0:1, 0:width])
             else:
-                nc.vector.tensor_copy(out=avg_sb[0:1, cols], in_=ps[0:1, :])
+                nc.vector.tensor_copy(out=avg_sb[0:1, cols], in_=ps[0:1, 0:width])
             nc.sync.dma_start(out=out_1_row[:, cols], in_=avg_sb[0:1, cols])

@@ -23,7 +23,9 @@ N_PASS = 40
 BLK = 4
 FLOPS = 2 * 128 * 20480 * 512
 
-SCALAR_INTERLEAVES = (9, 17, 25, 31, 35, 37, 38)
+SCALAR_INTERLEAVES = (21, 31, 35, 37, 38)
+TENSOR_INTERLEAVES = (9, 17, 25)
+WARM_BLK = 8
 LOOKAHEAD = 8
 LEAD = 2
 SC_FIRST = 4
@@ -86,8 +88,8 @@ def tile_gep_pa_kernel(tc, target_grad, bases0, bases1_bytes, bases1_scale, base
         nc.vector.memset(one[:], 1.0)
         warm = const.tile([P, 1], F32, name="warm")
         nc.scalar.activation(out=warm[:], in_=one[:], func=ACT.Abs_reciprocal_sqrt)
-        zeros = const.tile([P, N], BF16, name="zeros")
-        nc.vector.memset(zeros[:], 0.0)
+        ident_bf = const.tile([P, P], BF16, name="ident_bf")
+        make_identity(nc, ident_bf[:])
         idle_ps = psum_w.tile([P, N], F32, name="idle_ps")
         ident = const.tile([P, P], F32, name="ident")
         make_identity(nc, ident[:])
@@ -109,6 +111,7 @@ def tile_gep_pa_kernel(tc, target_grad, bases0, bases1_bytes, bases1_scale, base
         wids = {}
         grps = {}
         codes = {}
+        pbanks = {}
 
         def load(kind, idx):
             if kind == 1:
@@ -174,6 +177,25 @@ def tile_gep_pa_kernel(tc, target_grad, bases0, bases1_bytes, bases1_scale, base
                 )
             wids[s] = wid
 
+        def tensor_interleave(s):
+            src_v = raw[order[s]][:].rearrange("p (t n) -> p n t", t=PACK)
+            banks = []
+            for h in range(2):
+                pb = psum_t.tile([P, 2 * N], BF16, name="xt")
+                for q in range(2):
+                    n0 = (2 * h + q) * P
+                    nc.tensor.matmul(
+                        out=pb[:, q * N:(q + 1) * N].rearrange("p (n t) -> p n t", t=PACK),
+                        lhsT=ident_bf[:], rhs=src_v[:, n0:n0 + P, :], start=True, stop=True)
+                banks.append(pb)
+            pbanks[s] = banks
+
+        def tensor_interleave_out(s):
+            grp = grp_pool.tile([P, W], BF16, name="grp", align_bytes=64)
+            for h in range(2):
+                nc.scalar.copy(out=grp[:, h * 2 * N:(h + 1) * 2 * N], in_=pbanks[s][h][:])
+            grps[s] = grp
+
         def interleave(s):
             gp = order[s]
             src = wids[s] if s in wids else raw[gp]
@@ -218,7 +240,9 @@ def tile_gep_pa_kernel(tc, target_grad, bases0, bases1_bytes, bases1_scale, base
             if l == GROUP_PASSES[x] - 1:
                 finish_group(x)
             for w in range(WARMERS.get(s, 0)):
-                nc.tensor.matmul(out=idle_ps[:], lhsT=zeros[:, 0:P], rhs=zeros[:], start=True, stop=True)
+                wc, ws = gcodes[WARM_BLK]
+                nc.tensor.matmul_mx(out=idle_ps[:], lhsT=wc[:, 0:P].bitcast(FP8X4), lhsT_scale=ws[:, 0:P],
+                                    rhs=wc[:].bitcast(FP8X4), rhs_scale=ws[:], start=True, stop=True)
 
         ctx.enter_context(tc.manual_schedule())
         for it in range(-LOOKAHEAD - 2, N_PASS + 4):
@@ -236,14 +260,18 @@ def tile_gep_pa_kernel(tc, target_grad, bases0, bases1_bytes, bases1_scale, base
             for blk, s in first_need.items():
                 if s == it + 2:
                     transposes(blk)
+            if it + 3 in TENSOR_INTERLEAVES:
+                tensor_interleave(it + 3)
             if 0 <= it + 3 < N_PASS:
                 widen(it + 3)
             for blk, s in first_need.items():
                 if s == it - 1:
                     evacuate(blk)
+            if it + 2 in TENSOR_INTERLEAVES:
+                tensor_interleave_out(it + 2)
             if 0 <= it + 2 < N_PASS and it + 2 in SCALAR_INTERLEAVES:
                 interleave(it + 2)
-            if 0 <= it + 1 < N_PASS and it + 1 not in SCALAR_INTERLEAVES:
+            if 0 <= it + 1 < N_PASS and it + 1 not in SCALAR_INTERLEAVES and it + 1 not in TENSOR_INTERLEAVES:
                 interleave(it + 1)
             if 0 <= it < N_PASS:
                 quantize(it)

@@ -23,8 +23,8 @@ N_PASS = 40
 BLK = 4
 FLOPS = 2 * 128 * 20480 * 512
 
-SCALAR_INTERLEAVES = (21, 31, 35, 37, 38)
-TENSOR_INTERLEAVES = (9, 17, 25)
+SCALAR_INTERLEAVES = (9, 17, 21, 35, 38)
+TENSOR_INTERLEAVES = (25, 31, 37)
 WARM_BLK = 8
 LOOKAHEAD = 8
 LEAD = 2
@@ -90,7 +90,6 @@ def tile_gep_pa_kernel(tc, target_grad, bases0, bases1_bytes, bases1_scale, base
         nc.scalar.activation(out=warm[:], in_=one[:], func=ACT.Abs_reciprocal_sqrt)
         ident_bf = const.tile([P, P], BF16, name="ident_bf")
         make_identity(nc, ident_bf[:])
-        idle_ps = psum_w.tile([P, N], F32, name="idle_ps")
         ident = const.tile([P, P], F32, name="ident")
         make_identity(nc, ident[:])
 
@@ -181,7 +180,10 @@ def tile_gep_pa_kernel(tc, target_grad, bases0, bases1_bytes, bases1_scale, base
             src_v = raw[order[s]][:].rearrange("p (t n) -> p n t", t=PACK)
             banks = []
             for h in range(2):
-                pb = psum_t.tile([P, 2 * N], BF16, name="xt")
+                if h == 0:
+                    pb = psum_acc.tile([P, 2 * N], BF16, name="acc0")
+                else:
+                    pb = psum_w.tile([P, 2 * N], BF16, name="idle_ps")
                 for q in range(2):
                     n0 = (2 * h + q) * P
                     nc.tensor.matmul(
@@ -240,6 +242,10 @@ def tile_gep_pa_kernel(tc, target_grad, bases0, bases1_bytes, bases1_scale, base
             if l == GROUP_PASSES[x] - 1:
                 finish_group(x)
             for w in range(WARMERS.get(s, 0)):
+                if "idle" not in pbanks:
+                    idle_ps = psum_w.tile([P, N], F32, name="idle_ps")
+                    pbanks["idle"] = idle_ps
+                idle_ps = pbanks["idle"]
                 wc, ws = gcodes[WARM_BLK]
                 nc.tensor.matmul_mx(out=idle_ps[:], lhsT=wc[:, 0:P].bitcast(FP8X4), lhsT_scale=ws[:, 0:P],
                                     rhs=wc[:].bitcast(FP8X4), rhs_scale=ws[:], start=True, stop=True)

@@ -181,7 +181,7 @@ def tile_gep_pa_kernel(tc, target_grad, bases0, bases1_bytes, bases1_scale, base
             banks = []
             for h in range(2):
                 if h == 0:
-                    pb = psum_acc.tile([P, 2 * N], BF16, name="acc0")
+                    pb = psum_t.tile([P, 2 * N], BF16, name="xt")
                 else:
                     pb = psum_w.tile([P, 2 * N], BF16, name="idle_ps")
                 for q in range(2):
@@ -239,7 +239,7 @@ def tile_gep_pa_kernel(tc, target_grad, bases0, bases1_bytes, bases1_scale, base
                 start=(l == 0),
                 stop=(l == GROUP_PASSES[x] - 1),
             )
-            if l == GROUP_PASSES[x] - 1:
+            if l == GROUP_PASSES[x] - 1 and x != 0:
                 finish_group(x)
             for w in range(WARMERS.get(s, 0)):
                 if "idle" not in pbanks:
@@ -284,6 +284,8 @@ def tile_gep_pa_kernel(tc, target_grad, bases0, bases1_bytes, bases1_scale, base
             for blk, s in first_need.items():
                 if s == it - 2:
                     quantize_g(blk)
+            if it == N_PASS:
+                finish_group(0)
             if 0 <= it - 4 < N_PASS:
                 multiply(it - 4)
 

@@ -28,6 +28,8 @@ TENSOR_INTERLEAVES = (25, 31, 37)
 WARM_BLK = 8
 LOOKAHEAD = 8
 LEAD = 2
+EARLY_STEPS = 4
+EARLY_LAG = 3
 SC_FIRST = 4
 SC_REST_AFTER = 6
 WARMERS = {33: 2, 34: 2, 35: 2, 39: 3}
@@ -62,9 +64,11 @@ def tile_gep_pa_kernel(tc, target_grad, bases0, bases1_bytes, bases1_scale, base
 
     events = []
     for s, gp in enumerate(order):
-        events.append((s - (1.2 if group_of(gp)[0] == 1 else 0.0), 0, gp))
+        events.append((s - (2.2 if group_of(gp)[0] == 1 else 0.0), 0, gp))
+    lag = {}
     for blk, s in first_need.items():
-        events.append((s + 1.5, 1, blk))
+        lag[blk] = EARLY_LAG if s < EARLY_STEPS else 0
+        events.append((s + 1.5 + lag[blk], 1, blk))
     events = sorted(events)
 
     with ExitStack() as ctx:
@@ -73,8 +77,8 @@ def tile_gep_pa_kernel(tc, target_grad, bases0, bases1_bytes, bases1_scale, base
         byte_pool = ctx.enter_context(tc.tile_pool(name="bytes", bufs=6))
         graw_pool = ctx.enter_context(tc.tile_pool(name="graw", bufs=3))
         wid_pool = ctx.enter_context(tc.tile_pool(name="wid", bufs=4))
-        grp_pool = ctx.enter_context(tc.tile_pool(name="grp", bufs=5))
-        cq_pool = ctx.enter_context(tc.tile_pool(name="cq", bufs=10))
+        grp_pool = ctx.enter_context(tc.tile_pool(name="grp", bufs=4))
+        cq_pool = ctx.enter_context(tc.tile_pool(name="cq", bufs=6))
         ggrp_pool = ctx.enter_context(tc.tile_pool(name="ggrp", bufs=2))
         gq_pool = ctx.enter_context(tc.tile_pool(name="gq", bufs=1))
         psum_acc = ctx.enter_context(tc.psum_pool(name="psacc", bufs=1))
@@ -111,6 +115,13 @@ def tile_gep_pa_kernel(tc, target_grad, bases0, bases1_bytes, bases1_scale, base
         grps = {}
         codes = {}
         pbanks = {}
+        done = set()
+
+        def grp_cols(s, c0, c1):
+            if s // 2 not in grps:
+                pair = grp_pool.tile([P, 2 * W], BF16, name="grp", align_bytes=64)
+                grps[s // 2] = pair
+            return grps[s // 2][:, (s % 2) * W + c0:(s % 2) * W + c1]
 
         def load(kind, idx):
             if kind == 1:
@@ -193,49 +204,47 @@ def tile_gep_pa_kernel(tc, target_grad, bases0, bases1_bytes, bases1_scale, base
             pbanks[s] = banks
 
         def tensor_interleave_out(s):
-            grp = grp_pool.tile([P, W], BF16, name="grp", align_bytes=64)
             for h in range(2):
-                nc.scalar.copy(out=grp[:, h * 2 * N:(h + 1) * 2 * N], in_=pbanks[s][h][:])
-            grps[s] = grp
+                nc.scalar.copy(out=grp_cols(s, h * 2 * N, (h + 1) * 2 * N), in_=pbanks[s][h][:])
 
         def interleave(s):
             gp = order[s]
             src = wids[s] if s in wids else raw[gp]
-            grp = grp_pool.tile([P, W], BF16, name="grp", align_bytes=64)
-            dst_v = grp[:].rearrange("p (c i t) -> p c t i", i=4, t=PACK)
+            dst_v = grp_cols(s, 0, W).rearrange("p (c i t) -> p c t i", i=4, t=PACK)
             src_v = src[:].rearrange("p (t c i) -> p c t i", t=PACK, i=4)
             if s in SCALAR_INTERLEAVES:
                 nc.scalar.copy(out=dst_v, in_=src_v)
             else:
                 nc.vector.tensor_copy(out=dst_v, in_=src_v)
-            grps[s] = grp
 
-        def quantize(s):
-            cd = cq_pool.tile([P, N], U32, name="codes", align_bytes=64)
-            sl = cq_pool.tile([P, N], U8, name="scales", align_bytes=64)
-            nc.vector.quantize_mx(out=cd[:].bitcast(FP8X4), scales=sl[:], in_=grps[s][:])
-            codes[s] = (cd, sl)
+        def quantize(first, count):
+            if first // 2 not in codes:
+                cd = cq_pool.tile([P, 2 * N], U32, name="codes", align_bytes=64)
+                sl = cq_pool.tile([P, 2 * N], U8, name="scales", align_bytes=64)
+                codes[first // 2] = (cd, sl)
+            cd, sl = codes[first // 2]
+            cols = slice((first % 2) * N, (first % 2 + count) * N)
+            nc.vector.quantize_mx(out=cd[:, cols].bitcast(FP8X4), scales=sl[:, cols], in_=grp_cols(first, 0, count * W))
 
         def finish_group(x):
             cols = slice(x * N, (x + 1) * N)
             nc.scalar.activation(out=junk[:], in_=acc[x][:], func=ACT.Square, accum_out=ss[:, x:x + 1])
-            if x != 2:
-                nc.vector.tensor_copy(out=e_sb[:, cols], in_=acc[x][:])
             if x == 1:
-                nc.sync.dma_start(out=out_0[:, 0:2 * N], in_=e_sb[:, 0:2 * N])
+                nc.vector.tensor_copy(out=e_sb[:, cols], in_=acc[x][:])
 
         def multiply(s):
             gp = order[s]
             x, l = group_of(gp)
             gc, gs = gcodes[gp // BLK]
             a = gp % BLK
-            cd, sl = codes[s]
+            cd, sl = codes[s // 2]
+            cols = slice((s % 2) * N, (s % 2 + 1) * N)
             nc.tensor.matmul_mx(
                 out=acc[x][:],
                 lhsT=gc[:, a * P:(a + 1) * P].bitcast(FP8X4),
                 lhsT_scale=gs[:, a * P:(a + 1) * P],
-                rhs=cd[:].bitcast(FP8X4),
-                rhs_scale=sl[:],
+                rhs=cd[:, cols].bitcast(FP8X4),
+                rhs_scale=sl[:, cols],
                 start=(l == 0),
                 stop=(l == GROUP_PASSES[x] - 1),
             )
@@ -264,14 +273,14 @@ def tile_gep_pa_kernel(tc, target_grad, bases0, bases1_bytes, bases1_scale, base
                             nc.sync.dma_start(out=sc_b[:].rearrange("p (g t) -> p g t", t=PACK),
                                               in_=scale_view[:, SC_FIRST:GROUP_PASSES[1], :])
             for blk, s in first_need.items():
-                if s == it + 2:
+                if s + lag[blk] == it + 2:
                     transposes(blk)
             if it + 3 in TENSOR_INTERLEAVES:
                 tensor_interleave(it + 3)
             if 0 <= it + 3 < N_PASS:
                 widen(it + 3)
             for blk, s in first_need.items():
-                if s == it - 1:
+                if s + lag[blk] == it - 1:
                     evacuate(blk)
             if it + 2 in TENSOR_INTERLEAVES:
                 tensor_interleave_out(it + 2)
@@ -279,26 +288,32 @@ def tile_gep_pa_kernel(tc, target_grad, bases0, bases1_bytes, bases1_scale, base
                 interleave(it + 2)
             if 0 <= it + 1 < N_PASS and it + 1 not in SCALAR_INTERLEAVES and it + 1 not in TENSOR_INTERLEAVES:
                 interleave(it + 1)
-            if 0 <= it < N_PASS:
-                quantize(it)
+            if N_PASS - 2 <= it < N_PASS:
+                quantize(it, 1)
+            elif 0 <= it < N_PASS and it % 2 == 1:
+                quantize(it - 1, 2)
             for blk, s in first_need.items():
-                if s == it - 2:
+                if s + lag[blk] == it - 2:
                     quantize_g(blk)
             if it == N_PASS:
                 finish_group(0)
-            if 0 <= it - 4 < N_PASS:
-                multiply(it - 4)
+            for s in range(N_PASS):
+                if s not in done and s <= it - 4 and order[s] // BLK in gcodes and (s == 0 or s - 1 in done):
+                    multiply(s)
+                    done.add(s)
 
         ss01 = const.tile([P, 1], F32, name="ss01")
         nc.vector.tensor_tensor(out=ss01[:], in0=ss[:, 0:1], in1=ss[:, 1:2], op=ALU.add)
         m = const.tile([P, 1], F32, name="m")
         nc.vector.tensor_scalar(out=m[:], in0=ss[:, 2:3], scalar1=ss01[:, 0:1], scalar2=1.0, op0=ALU.add, op1=ALU.max)
+        nc.vector.tensor_copy(out=e_sb[:, 0:N], in_=acc[0][:])
+        nc.sync.dma_start(out=out_0[:, 0:2 * N], in_=e_sb[:, 0:2 * N])
         cw = const.tile([P, 1], F32, name="cw")
         nc.scalar.activation(out=cw[:], in_=m[:], func=ACT.Abs_reciprocal_sqrt, scale=16384.0)
         nc.scalar.copy(out=e_sb[:, 2 * N:3 * N], in_=acc[2][:])
         nc.sync.dma_start(out=out_0[:, 2 * N:3 * N], in_=e_sb[:, 2 * N:3 * N])
         out_1_row = out_1.rearrange("(o n) -> o n", o=1)
-        pieces = ((0, N), (N, N), (2 * N, N // 2), (2 * N + N // 2, N // 2))
+        pieces = ((N, N), (0, N), (2 * N, N // 2), (2 * N + N // 2, N // 2))
         for i, (c0, width) in enumerate(pieces):
             cols = slice(c0, c0 + width)
             ps = psum_t.tile([P, N], F32, name="xt")

@@ -210,8 +210,8 @@ def tile_gep_pa_kernel(tc, target_grad, bases0, bases1_bytes, bases1_scale, base
         def interleave(s):
             gp = order[s]
             src = wids[s] if s in wids else raw[gp]
-            dst_v = grp_cols(s, 0, W).rearrange("p (c i t) -> p c t i", i=4, t=PACK)
-            src_v = src[:].rearrange("p (t c i) -> p c t i", t=PACK, i=4)
+            dst_v = grp_cols(s, 0, W).rearrange("p (c i t) -> p c t i", i=8, t=PACK)
+            src_v = src[:].rearrange("p (t c i) -> p c t i", t=PACK, i=8)
             if s in SCALAR_INTERLEAVES:
                 nc.scalar.copy(out=dst_v, in_=src_v)
             else:

from contextlib import ExitStack

import concourse.mybir as mybir
from concourse.masks import make_identity

F32 = mybir.dt.float32
BF16 = mybir.dt.bfloat16
U32 = mybir.dt.uint32
U8 = mybir.dt.uint8
FP8 = mybir.dt.float8_e4m3fn
FP8X4 = mybir.dt.float8_e4m3fn_x4
ACT = mybir.ActivationFunctionType
ALU = mybir.AluOpType

P = 128
PACK = 4
K_PASS = P * PACK
N = 512
W = PACK * N
GROUP_FIRST = (0, 8, 26)
GROUP_PASSES = (8, 18, 14)
N_PASS = 40
BLK = 4
FLOPS = 2 * 128 * 20480 * 512

SCALAR_INTERLEAVES = (9, 17, 21, 35, 38)
TENSOR_INTERLEAVES = (25, 31, 37)
WARM_BLK = 8
LOOKAHEAD = 8
LEAD = 2
EARLY_STEPS = 4
EARLY_LAG = 3
SC_FIRST = 4
SC_REST_AFTER = 6
WARMERS = {33: 2, 34: 2, 35: 2, 39: 3}


def pass_order():
    plain = list(range(0, 8)) + list(range(26, 40))
    coded = list(range(8, 26))
    order = plain[:LEAD]
    rest = plain[LEAD:]
    for i in range(len(coded)):
        order.append(coded[i])
        order.append(rest[i])
    order.extend(rest[len(coded):])
    return order


def group_of(gp):
    x = 0
    for g in range(3):
        if gp >= GROUP_FIRST[g]:
            x = g
    return x, gp - GROUP_FIRST[x]


def tile_gep_pa_kernel(tc, target_grad, bases0, bases1_bytes, bases1_scale, bases2, out_0, out_1):
    nc = tc.nc
    order = pass_order()
    first_need = {}
    for s, gp in enumerate(order):
        first_need.setdefault(gp // BLK, s)

    events = []
    for s, gp in enumerate(order):
        events.append((s - (2.2 if group_of(gp)[0] == 1 else 0.0), 0, gp))
    lag = {}
    for blk, s in first_need.items():
        lag[blk] = EARLY_LAG if s < EARLY_STEPS else 0
        events.append((s + 1.5 + lag[blk], 1, blk))
    events = sorted(events)

    with ExitStack() as ctx:
        const = ctx.enter_context(tc.tile_pool(name="const", bufs=1))
        braw_pool = ctx.enter_context(tc.tile_pool(name="braw", bufs=6))
        byte_pool = ctx.enter_context(tc.tile_pool(name="bytes", bufs=6))
        graw_pool = ctx.enter_context(tc.tile_pool(name="graw", bufs=3))
        wid_pool = ctx.enter_context(tc.tile_pool(name="wid", bufs=4))
        grp_pool = ctx.enter_context(tc.tile_pool(name="grp", bufs=4))
        cq_pool = ctx.enter_context(tc.tile_pool(name="cq", bufs=6))
        ggrp_pool = ctx.enter_context(tc.tile_pool(name="ggrp", bufs=2))
        gq_pool = ctx.enter_context(tc.tile_pool(name="gq", bufs=1))
        psum_acc = ctx.enter_context(tc.psum_pool(name="psacc", bufs=1))
        psum_t = ctx.enter_context(tc.psum_pool(name="pst", bufs=4))
        psum_w = ctx.enter_context(tc.psum_pool(name="psw", bufs=1))

        scale_view = bases1_scale.rearrange("(g p t) o -> p g (t o)", p=P, t=PACK)
        sc_a = const.tile([P, SC_FIRST * PACK], F32, name="sc_a")
        sc_b = const.tile([P, (GROUP_PASSES[1] - SC_FIRST) * PACK], F32, name="sc_b")
        one = const.tile([P, 1], F32, name="one")
        nc.vector.memset(one[:], 1.0)
        warm = const.tile([P, 1], F32, name="warm")
        nc.scalar.activation(out=warm[:], in_=one[:], func=ACT.Abs_reciprocal_sqrt)
        ident_bf = const.tile([P, P], BF16, name="ident_bf")
        make_identity(nc, ident_bf[:])
        ident = const.tile([P, P], F32, name="ident")
        make_identity(nc, ident[:])

        e_sb = const.tile([P, 3 * N], F32, name="e_sb")
        avg_sb = const.tile([P, 3 * N], F32, name="avg_sb")
        junk = const.tile([P, N], F32, name="junk")
        ss = const.tile([P, 4], F32, name="ss")
        acc = []
        for x in range(3):
            acc_x = psum_acc.tile([P, N], F32, name="acc%d" % x)
            acc.append(acc_x)

        raw = {}
        graw = {}
        xts = {}
        ggrps = {}
        gcodes = {}
        wids = {}
        grps = {}
        codes = {}
        pbanks = {}
        done = set()

        def grp_cols(s, c0, c1):
            if s // 2 not in grps:
                pair = grp_pool.tile([P, 2 * W], BF16, name="grp", align_bytes=64)
                grps[s // 2] = pair
            return grps[s // 2][:, (s % 2) * W + c0:(s % 2) * W + c1]

        def load(kind, idx):
            if kind == 1:
                t = graw_pool.tile([P, BLK * K_PASS], BF16, name="graw")
                nc.sync.dma_start(out=t[:], in_=target_grad[:, idx * BLK * K_PASS:(idx + 1) * BLK * K_PASS])
                graw[idx] = t
                return
            x, l = group_of(idx)
            rows = slice(l * K_PASS, (l + 1) * K_PASS)
            if x == 1:
                t = byte_pool.tile([P, W], U8, name="b1bytes")
                nc.sync.dma_start(out=t[:], in_=bases1_bytes[rows, :].rearrange("(p j) n -> p (j n)", j=PACK))
            else:
                src = bases0 if x == 0 else bases2
                t = braw_pool.tile([P, W], BF16, name="braw")
                nc.sync.dma_start(out=t[:], in_=src[rows, :].rearrange("(p j) n -> p (j n)", j=PACK))
            raw[idx] = t

        def transposes(blk):
            words = graw[blk][:].bitcast(F32)
            banks = []
            for h in range(2):
                xt = psum_t.tile([P, N], F32, name="xt")
                for a in range(2):
                    for u in range(2):
                        base = 256 * (2 * h + a)
                        nc.tensor.transpose(
                            out=xt[:, (2 * a + u) * P:(2 * a + u + 1) * P],
                            in_=words[:, base + u:base + 256:2],
                            identity=ident[:],
                        )
                banks.append(xt)
            xts[blk] = banks

        def evacuate(blk):
            ggrp = ggrp_pool.tile([P, BLK * K_PASS], BF16, name="ggrp", align_bytes=64)
            for h in range(2):
                nc.scalar.copy(
                    out=ggrp[:, h * 1024:(h + 1) * 1024].bitcast(F32).rearrange("p (a r u) -> p a r u", a=2, u=2),
                    in_=xts[blk][h][:].rearrange("p (a u r) -> p a r u", a=2, u=2),
                )
            ggrps[blk] = ggrp

        def quantize_g(blk):
            gc = gq_pool.tile([P, BLK * P], U32, name="gc%d" % blk, align_bytes=64)
            gs = gq_pool.tile([P, BLK * P], U8, name="gs%d" % blk, align_bytes=64)
            nc.vector.quantize_mx(out=gc[:].bitcast(FP8X4), scales=gs[:], in_=ggrps[blk][:])
            gcodes[blk] = (gc, gs)

        def widen(s):
            gp = order[s]
            x, l = group_of(gp)
            if x != 1:
                return
            wid = wid_pool.tile([P, W], BF16, name="wid")
            for j in range(PACK):
                nc.scalar.activation(
                    out=wid[:, j * N:(j + 1) * N],
                    in_=raw[gp][:, j * N:(j + 1) * N].bitcast(FP8),
                    func=ACT.Copy,
                    scale=(sc_a[:, l * PACK + j:l * PACK + j + 1] if l < SC_FIRST
                           else sc_b[:, (l - SC_FIRST) * PACK + j:(l - SC_FIRST) * PACK + j + 1]),
                )
            wids[s] = wid

        def tensor_interleave(s):
            src_v = raw[order[s]][:].rearrange("p (t n) -> p n t", t=PACK)
            banks = []
            for h in range(2):
                if h == 0:
                    pb = psum_t.tile([P, 2 * N], BF16, name="xt")
                else:
                    pb = psum_w.tile([P, 2 * N], BF16, name="idle_ps")
                for q in range(2):
                    n0 = (2 * h + q) * P
                    nc.tensor.matmul(
                        out=pb[:, q * N:(q + 1) * N].rearrange("p (n t) -> p n t", t=PACK),
                        lhsT=ident_bf[:], rhs=src_v[:, n0:n0 + P, :], start=True, stop=True)
                banks.append(pb)
            pbanks[s] = banks

        def tensor_interleave_out(s):
            for h in range(2):
                nc.scalar.copy(out=grp_cols(s, h * 2 * N, (h + 1) * 2 * N), in_=pbanks[s][h][:])

        def interleave(s):
            gp = order[s]
            src = wids[s] if s in wids else raw[gp]
            dst_v = grp_cols(s, 0, W).rearrange("p (c i t) -> p c t i", i=8, t=PACK)
            src_v = src[:].rearrange("p (t c i) -> p c t i", t=PACK, i=8)
            if s in SCALAR_INTERLEAVES:
                nc.scalar.copy(out=dst_v, in_=src_v)
            else:
                nc.vector.tensor_copy(out=dst_v, in_=src_v)

        def quantize(first, count):
            if first // 2 not in codes:
                cd = cq_pool.tile([P, 2 * N], U32, name="codes", align_bytes=64)
                sl = cq_pool.tile([P, 2 * N], U8, name="scales", align_bytes=64)
                codes[first // 2] = (cd, sl)
            cd, sl = codes[first // 2]
            cols = slice((first % 2) * N, (first % 2 + count) * N)
            nc.vector.quantize_mx(out=cd[:, cols].bitcast(FP8X4), scales=sl[:, cols], in_=grp_cols(first, 0, count * W))

        def finish_group(x):
            cols = slice(x * N, (x + 1) * N)
            nc.scalar.activation(out=junk[:], in_=acc[x][:], func=ACT.Square, accum_out=ss[:, x:x + 1])
            if x == 1:
                nc.vector.tensor_copy(out=e_sb[:, cols], in_=acc[x][:])

        def multiply(s):
            gp = order[s]
            x, l = group_of(gp)
            gc, gs = gcodes[gp // BLK]
            a = gp % BLK
            cd, sl = codes[s // 2]
            cols = slice((s % 2) * N, (s % 2 + 1) * N)
            nc.tensor.matmul_mx(
                out=acc[x][:],
                lhsT=gc[:, a * P:(a + 1) * P].bitcast(FP8X4),
                lhsT_scale=gs[:, a * P:(a + 1) * P],
                rhs=cd[:, cols].bitcast(FP8X4),
                rhs_scale=sl[:, cols],
                start=(l == 0),
                stop=(l == GROUP_PASSES[x] - 1),
            )
            if l == GROUP_PASSES[x] - 1 and x != 0:
                finish_group(x)
            for w in range(WARMERS.get(s, 0)):
                if "idle" not in pbanks:
                    idle_ps = psum_w.tile([P, N], F32, name="idle_ps")
                    pbanks["idle"] = idle_ps
                idle_ps = pbanks["idle"]
                wc, ws = gcodes[WARM_BLK]
                nc.tensor.matmul_mx(out=idle_ps[:], lhsT=wc[:, 0:P].bitcast(FP8X4), lhsT_scale=ws[:, 0:P],
                                    rhs=wc[:].bitcast(FP8X4), rhs_scale=ws[:], start=True, stop=True)

        ctx.enter_context(tc.manual_schedule())
        for it in range(-LOOKAHEAD - 2, N_PASS + 4):
            for e_i, (when, kind, idx) in enumerate(events):
                if int(when + 100) - 100 - LOOKAHEAD == it:
                    load(kind, idx)
                    if e_i == 0:
                        with nc.allow_non_contiguous_dma(reason="16-byte runs of scales"):
                            nc.sync.dma_start(out=sc_a[:].rearrange("p (g t) -> p g t", t=PACK),
                                              in_=scale_view[:, 0:SC_FIRST, :])
                    if e_i == SC_REST_AFTER:
                        with nc.allow_non_contiguous_dma(reason="16-byte runs of scales"):
                            nc.sync.dma_start(out=sc_b[:].rearrange("p (g t) -> p g t", t=PACK),
                                              in_=scale_view[:, SC_FIRST:GROUP_PASSES[1], :])
            for blk, s in first_need.items():
                if s + lag[blk] == it + 2:
                    transposes(blk)
            if it + 3 in TENSOR_INTERLEAVES:
                tensor_interleave(it + 3)
            if 0 <= it + 3 < N_PASS:
                widen(it + 3)
            for blk, s in first_need.items():
                if s + lag[blk] == it - 1:
                    evacuate(blk)
            if it + 2 in TENSOR_INTERLEAVES:
                tensor_interleave_out(it + 2)
            if 0 <= it + 2 < N_PASS and it + 2 in SCALAR_INTERLEAVES:
                interleave(it + 2)
            if 0 <= it + 1 < N_PASS and it + 1 not in SCALAR_INTERLEAVES and it + 1 not in TENSOR_INTERLEAVES:
                interleave(it + 1)
            if N_PASS - 2 <= it < N_PASS:
                quantize(it, 1)
            elif 0 <= it < N_PASS and it % 2 == 1:
                quantize(it - 1, 2)
            for blk, s in first_need.items():
                if s + lag[blk] == it - 2:
                    quantize_g(blk)
            if it == N_PASS:
                finish_group(0)
            for s in range(N_PASS):
                if s not in done and s <= it - 4 and order[s] // BLK in gcodes and (s == 0 or s - 1 in done):
                    multiply(s)
                    done.add(s)

        ss01 = const.tile([P, 1], F32, name="ss01")
        nc.vector.tensor_tensor(out=ss01[:], in0=ss[:, 0:1], in1=ss[:, 1:2], op=ALU.add)
        m = const.tile([P, 1], F32, name="m")
        nc.vector.tensor_scalar(out=m[:], in0=ss[:, 2:3], scalar1=ss01[:, 0:1], scalar2=1.0, op0=ALU.add, op1=ALU.max)
        nc.vector.tensor_copy(out=e_sb[:, 0:N], in_=acc[0][:])
        nc.sync.dma_start(out=out_0[:, 0:2 * N], in_=e_sb[:, 0:2 * N])
        cw = const.tile([P, 1], F32, name="cw")
        nc.scalar.activation(out=cw[:], in_=m[:], func=ACT.Abs_reciprocal_sqrt, scale=16384.0)
        nc.scalar.copy(out=e_sb[:, 2 * N:3 * N], in_=acc[2][:])
        nc.sync.dma_start(out=out_0[:, 2 * N:3 * N], in_=e_sb[:, 2 * N:3 * N])
        out_1_row = out_1.rearrange("(o n) -> o n", o=1)
        pieces = ((N, N), (0, N), (2 * N, N // 2), (2 * N + N // 2, N // 2))
        for i, (c0, width) in enumerate(pieces):
            cols = slice(c0, c0 + width)
            ps = psum_t.tile([P, N], F32, name="xt")
            nc.tensor.matmul(out=ps[:, 0:width], lhsT=cw[:, 0:1].to_broadcast([P, P]), rhs=e_sb[:, cols], start=True, stop=True)
            if i % 2 == 1:
                nc.scalar.copy(out=avg_sb[0:1, cols], in_=ps[0:1, 0:width])
            else:
                nc.vector.tensor_copy(out=avg_sb[0:1, cols], in_=ps[0:1, 0:width])
            nc.sync.dma_start(out=out_1_row[:, cols], in_=avg_sb[0:1, cols])
